import numpy as np
import ml_dtypes


def mxq(x, axis, fmt="e4m3"):
    dtype, down = {"e4m3": (ml_dtypes.float8_e4m3fn, 7), "e5m2": (ml_dtypes.float8_e5m2, 14)}[fmt]
    v = np.moveaxis(np.asarray(x, np.float32).astype(ml_dtypes.bfloat16).astype(np.float64), axis, -1)
    blocks = v.reshape(v.shape[:-1] + (-1, 32))
    amax = np.abs(blocks).max(-1, keepdims=True)
    byte = np.maximum(np.where(amax > 0, np.frexp(amax)[1] - 1 + 127, 0) - down, 1)
    scale = np.exp2(byte - 127.0)
    codes = (blocks / scale).astype(np.float32).astype(dtype).astype(np.float64)
    return np.moveaxis((codes * scale).reshape(v.shape), -1, axis)


WIDE = False


def mx_kscale(k):
    if not WIDE:
        return np.ones(k)
    levels = np.array([10, -10, 5, -5, 0])
    if k % 512:
        return np.exp2(np.random.permutation(np.resize(levels, k // 32))).repeat(32)
    a = np.empty((k // 512, 16))
    for p in range(k // 512):
        a[p, :8] = np.random.permutation(np.resize(levels, 8))
        for g in range(8):
            far = levels[np.abs(levels - a[p, g]) >= 10]
            a[p, g + 8] = far[np.random.randint(len(far))]
    return np.exp2(a.ravel()).repeat(32)


BF16 = ml_dtypes.bfloat16


def bf(x):
    return np.asarray(x, np.float32).astype(BF16)


def f64(x):
    return np.asarray(x).astype(np.float64)


N, H, O, L = 1024, 512, 512, 4


def represent(h):
    n = h.shape[0]
    total = np.sum(h, axis=0, keepdims=True)
    return (n * h - total) / (n - 1)


def sigmoid(v):
    return 1.0 / (1.0 + np.exp(-v))


def setup_inputs():
    t = mx_kscale(H)
    mu = np.random.standard_normal(H)
    return {"h": bf((np.random.standard_normal((N, H)) * 1.2 + mu) * t),
            "w": bf(np.random.standard_normal((H, H)) * 0.6 / np.sqrt(H) * t[:, None] / t[None, :]),
            "w_ff": bf(np.random.standard_normal((O, H)) * 0.6 / np.sqrt(H) / t[None, :]),
            "b_ff": bf(np.random.standard_normal(O) * 0.3)}


def reference(h, w, w_ff, b_ff):
    h = f64(h)
    r = represent(h)
    f = mxq(r, 1, "e4m3") @ mxq(f64(w), 1, "e4m3").T
    h_new = f + h
    return sigmoid((mxq(h_new, 1, "e4m3") @ mxq(f64(w_ff), 1, "e4m3").T) + f64(b_ff))

@@ -1,0 +1,318 @@
+from contextlib import ExitStack
+
+import concourse.mybir as mybir
+from concourse.masks import make_identity
+
+N_ROWS, HID, OUT = 1024, 512, 512
+FLOPS = 2 * N_ROWS * HID * HID + 2 * N_ROWS * HID * OUT
+
+F32 = mybir.dt.float32
+BF16 = mybir.dt.bfloat16
+U32 = mybir.dt.uint32
+U8 = mybir.dt.uint8
+FP8X4 = mybir.dt.float8_e4m3fn_x4
+ALU = mybir.AluOpType
+ACT = mybir.ActivationFunctionType
+AX = mybir.AxisListType
+
+P = 128
+NT = N_ROWS // P
+NQ = NT // 2
+W2 = 2 * P
+
+
+def tile_differ_amplifier_pa_kernel(tc, h, w, w_ff, b_ff, out):
+    nc = tc.nc
+    with ExitStack() as ctx:
+        keep = ctx.enter_context(tc.tile_pool(name="keep", bufs=1))
+        work = ctx.enter_context(tc.tile_pool(name="work", bufs=4))
+        psum = ctx.enter_context(tc.psum_pool(name="psum", bufs=8))
+
+        h_view = h.rearrange("(p j) k -> p j k", j=NT)
+        out_view = out.rearrange("(p j) o -> p j o", j=NT)
+
+        h_sb = []
+        for q in range(NQ):
+            h_pair = keep.tile([P, 2, HID], BF16, name="h_sb%d" % q)
+            if q < NQ - 1:
+                nc.sync.dma_start(out=h_pair[:], in_=h_view[:, 2 * q : 2 * q + 2, :])
+            else:
+                for jj in range(2):
+                    nc.sync.dma_start(out=h_pair[:, jj, :], in_=h_view[:, 2 * q + jj, :])
+            h_sb.append(h_pair)
+        wt_sb = {}
+        for key, src in (("w", w), ("f", w_ff)):
+            src_view = src.rearrange("(i p) k -> p i k", p=P)
+            for i2 in range(2):
+                w_pair = keep.tile([P, 2, HID], BF16, name="w_sb_%s%d" % (key, i2))
+                nc.sync.dma_start(out=w_pair[:], in_=src_view[:, 2 * i2 : 2 * i2 + 2, :])
+                wt_sb[(key, i2)] = w_pair
+        bias_bf = keep.tile([P, OUT], BF16, name="bias_bf")
+        nc.sync.dma_start(out=bias_bf[:], in_=b_ff.partition_broadcast(P))
+
+        ident_bf = keep.tile([P, P], BF16, name="ident_bf")
+        make_identity(nc, ident_bf[:])
+        ident_f32 = keep.tile([P, P], F32, name="ident_f32")
+        make_identity(nc, ident_f32[:])
+        ones = keep.tile([P, HID], BF16, name="ones")
+        nc.vector.memset(ones[:], 1.0)
+        warm_in = keep.tile([P, 1], F32, name="warm_in")
+        nc.vector.memset(warm_in[:], 0.0)
+        warm_out = keep.tile([P, 1], F32, name="warm_out")
+        nc.scalar.activation(out=warm_out[:], in_=warm_in[:], func=ACT.Sigmoid)
+
+        ctx.enter_context(tc.manual_schedule())
+
+        warm_ps = psum.tile([P, HID], F32, tag="bank", name="warm_ps")
+        for rep in range(4):
+            nc.tensor.matmul(warm_ps[:], lhsT=ones[:, 0:P], rhs=ones[:], start=True, stop=True)
+        tot_ps = psum.tile([P, 96], F32, tag="bank", name="tot_ps")
+        tot_sb = keep.tile([P, 4], F32, name="tot_sb")
+        c_sb = keep.tile([P, 4], F32, name="c_sb")
+        hT_ps = {}
+        wT_ps = {}
+        wg = {}
+        codes = {}
+        scales = {}
+        for key in ("w", "f"):
+            codes[key] = keep.tile([P, HID], U32, name="codes_%s" % key, align_bytes=64)
+            scales[key] = keep.tile([P, HID], U8, name="scales_%s" % key, align_bytes=64)
+        rg = []
+        r_codes = []
+        r_scales = []
+        hn = []
+        hng = []
+        n_codes = []
+        n_scales = []
+        for q in range(NQ):
+            rg.append(keep.tile([P, W2, 4], BF16, name="rg%d" % q, align_bytes=64))
+            r_codes.append(keep.tile([P, W2], U32, name="r_codes%d" % q, align_bytes=64))
+            r_scales.append(keep.tile([P, W2], U8, name="r_scales%d" % q, align_bytes=64))
+            hn.append(keep.tile([P, 2, HID], BF16, name="hn%d" % q))
+            hng.append(keep.tile([P, W2, 4], BF16, name="hng%d" % q, align_bytes=64))
+            n_codes.append(keep.tile([P, W2], U32, name="n_codes%d" % q, align_bytes=64))
+            n_scales.append(keep.tile([P, W2], U8, name="n_scales%d" % q, align_bytes=64))
+        f_ps = {}
+        hnT_ps = {}
+        o_ps = {}
+        z_sb = {}
+
+        def sums(q):
+            for jj in range(2):
+                for t in range(4):
+                    col = 2 * (4 * (2 * q + jj) + t)
+                    nc.tensor.matmul(
+                        tot_ps[:, col : col + 32], lhsT=h_sb[q][:, jj, t:HID:4], rhs=ones[:, 0:32], start=True, stop=True
+                    )
+
+        def turn_h(q):
+            hT_ps[q] = psum.tile([P, 4, W2], BF16, tag="bank", name="hT_ps")
+            for jj in range(2):
+                for t in range(4):
+                    nc.tensor.transpose(hT_ps[q][:, t, jj * P : (jj + 1) * P], h_sb[q][:, jj, t:HID:4], ident_bf[:])
+
+        def total():
+            nc.vector.tensor_reduce(
+                out=tot_sb[:], in_=tot_ps[:, 0:64].rearrange("p (j t z) -> p t j z", t=4, z=2)[:, :, :, 0], axis=AX.X, op=ALU.add
+            )
+            nc.vector.tensor_scalar_mul(out=c_sb[:], in0=tot_sb[:], scalar1=-1.0 / (N_ROWS - 1))
+
+        def turn_w(key, i2):
+            wT_ps[(key, i2)] = psum.tile([P, 2, W2], F32, tag="bank", name="wT_ps")
+            for i in range(2):
+                words = wt_sb[(key, i2)][:, i, :].bitcast(F32)
+                for u in range(2):
+                    nc.tensor.transpose(
+                        wT_ps[(key, i2)][:, u, i * P : (i + 1) * P], words[:, u : HID // 2 : 2], ident_f32[:]
+                    )
+
+        def copy_w(key, i2):
+            wg[(key, i2)] = keep.tile([P, W2, 4], BF16, name="wg_%s%d" % (key, i2), align_bytes=64)
+            nc.scalar.copy(out=wg[(key, i2)][:].bitcast(F32), in_=wT_ps[(key, i2)][:].rearrange("p u o -> p o u"))
+
+        def quant_w(key, i2):
+            cols = slice(i2 * W2, (i2 + 1) * W2)
+            nc.vector.quantize_mx(
+                out=codes[key][:, cols].bitcast(FP8X4),
+                scales=scales[key][:, cols],
+                in_=wg[(key, i2)][:].rearrange("p o t -> p (o t)"),
+            )
+
+        def centre(q):
+            nc.vector.scalar_tensor_tensor(
+                out=rg[q][:],
+                in0=hT_ps[q][:].rearrange("p t n -> p n t"),
+                scalar=float(N_ROWS) / (N_ROWS - 1),
+                in1=c_sb[:].unsqueeze(1).to_broadcast([P, W2, 4]),
+                op0=ALU.mult,
+                op1=ALU.add,
+            )
+
+        def centre_s(q):
+            for t in range(4):
+                nc.scalar.activation(
+                    out=rg[q][:, :, t],
+                    in_=hT_ps[q][:, t, :],
+                    func=ACT.Identity,
+                    scale=float(N_ROWS) / (N_ROWS - 1),
+                    bias=c_sb[:, t : t + 1],
+                )
+
+        def quant_r(q):
+            nc.vector.quantize_mx(
+                out=r_codes[q][:].bitcast(FP8X4), scales=r_scales[q][:], in_=rg[q][:].rearrange("p n t -> p (n t)")
+            )
+
+        def mm1(j):
+            q, jj = divmod(j, 2)
+            rows = slice(jj * P, (jj + 1) * P)
+            f_ps[j] = psum.tile([P, HID], F32, tag="bank", name="f_ps")
+            nc.tensor.matmul_mx(
+                out=f_ps[j][:],
+                lhsT=r_codes[q][:, rows].bitcast(FP8X4),
+                lhsT_scale=r_scales[q][:, rows],
+                rhs=codes["w"][:].bitcast(FP8X4),
+                rhs_scale=scales["w"][:],
+                start=True,
+                stop=True,
+            )
+
+        def add_h(j):
+            q, jj = divmod(j, 2)
+            nc.vector.tensor_tensor(out=hn[q][:, jj, :], in0=f_ps[j][:], in1=h_sb[q][:, jj, :], op=ALU.add)
+
+        def turn_n(q):
+            hnT_ps[q] = psum.tile([P, 2, W2], F32, tag="bank", name="hnT_ps")
+            for jj in range(2):
+                words = hn[q][:, jj, :].bitcast(F32)
+                for u in range(2):
+                    nc.tensor.transpose(hnT_ps[q][:, u, jj * P : (jj + 1) * P], words[:, u : HID // 2 : 2], ident_f32[:])
+
+        def copy_n(q):
+            nc.scalar.copy(out=hng[q][:].bitcast(F32), in_=hnT_ps[q][:].rearrange("p u n -> p n u"))
+
+        def quant_n(q):
+            nc.vector.quantize_mx(
+                out=n_codes[q][:].bitcast(FP8X4), scales=n_scales[q][:], in_=hng[q][:].rearrange("p n t -> p (n t)")
+            )
+
+        def turn_n1(j):
+            q, jj = divmod(j, 2)
+            hnT_ps[(q, jj)] = psum.tile([P, 2, P], F32, tag="bank", name="hnT1_ps")
+            words = hn[q][:, jj, :].bitcast(F32)
+            for u in range(2):
+                nc.tensor.transpose(hnT_ps[(q, jj)][:, u, :], words[:, u : HID // 2 : 2], ident_f32[:])
+
+        def copy_n1(j):
+            q, jj = divmod(j, 2)
+            nc.scalar.copy(
+                out=hng[q][:, jj * P : (jj + 1) * P, :].bitcast(F32), in_=hnT_ps[(q, jj)][:].rearrange("p u n -> p n u")
+            )
+
+        def quant_n1(j):
+            q, jj = divmod(j, 2)
+            rows = slice(jj * P, (jj + 1) * P)
+            nc.vector.quantize_mx(
+                out=n_codes[q][:, rows].bitcast(FP8X4),
+                scales=n_scales[q][:, rows],
+                in_=hng[q][:, rows, :].rearrange("p n t -> p (n t)"),
+            )
+
+        def mm2(j):
+            q, jj = divmod(j, 2)
+            rows = slice(jj * P, (jj + 1) * P)
+            o_ps[j] = psum.tile([P, OUT], F32, tag="bank", name="o_ps")
+            nc.tensor.matmul_mx(
+                out=o_ps[j][:],
+                lhsT=n_codes[q][:, rows].bitcast(FP8X4),
+                lhsT_scale=n_scales[q][:, rows],
+                rhs=codes["f"][:].bitcast(FP8X4),
+                rhs_scale=scales["f"][:],
+                start=True,
+                stop=True,
+            )
+
+        def finish(j, c0=0, c1=OUT):
+            z = keep.tile([P, c1 - c0], F32, name="z%d_%d" % (j, c0))
+            nc.vector.tensor_tensor(out=z[:], in0=o_ps[j][:, c0:c1], in1=bias_bf[:, c0:c1], op=ALU.add)
+            y = keep.tile([P, c1 - c0], F32, name="y%d_%d" % (j, c0))
+            nc.scalar.activation(out=y[:], in_=z[:], func=ACT.Sigmoid)
+            nc.sync.dma_start(out=out_view[:, j, c0:c1], in_=y[:])
+
+        sums(0)
+        sums(1)
+        turn_h(0)
+        sums(2)
+        sums(3)
+        total()
+        turn_h(1)
+        centre(0)
+        turn_w("w", 0)
+        copy_w("w", 0)
+        turn_w("w", 1)
+        copy_w("w", 1)
+        centre(1)
+        turn_h(3)
+        centre_s(3)
+        turn_h(2)
+        quant_w("w", 0)
+        quant_w("w", 1)
+        quant_r(0)
+        centre(2)
+        quant_r(1)
+        turn_w("f", 0)
+        copy_w("f", 0)
+        turn_w("f", 1)
+        copy_w("f", 1)
+        mm1(0)
+        mm1(1)
+        mm1(2)
+        mm1(3)
+        add_h(0)
+        add_h(1)
+        quant_r(2)
+        mm1(4)
+        mm1(5)
+        turn_n(0)
+        copy_n(0)
+        add_h(2)
+        add_h(3)
+        quant_r(3)
+        mm1(6)
+        mm1(7)
+        turn_n(1)
+        copy_n(1)
+        add_h(4)
+        add_h(5)
+        turn_n(2)
+        copy_n(2)
+        quant_w("f", 0)
+        quant_w("f", 1)
+        quant_n(0)
+        mm2(0)
+        mm2(1)
+        add_h(6)
+        turn_n1(6)
+        copy_n1(6)
+        add_h(7)
+        turn_n1(7)
+        copy_n1(7)
+        quant_n(1)
+        mm2(2)
+        mm2(3)
+        finish(0)
+        finish(1)
+        quant_n(2)
+        quant_n1(6)
+        mm2(4)
+        mm2(5)
+        finish(2)
+        quant_n1(7)
+        mm2(6)
+        mm2(7)
+        finish(3)
+        finish(4)
+        finish(5)
+        finish(6)
+        finish(7, 0, OUT // 2)
+        finish(7, OUT // 2, OUT)

@@ -48,7 +48,6 @@ def tile_differ_amplifier_pa_kernel(tc, h, w, w_ff, b_ff, out):
                 nc.sync.dma_start(out=w_pair[:], in_=src_view[:, 2 * i2 : 2 * i2 + 2, :])
                 wt_sb[(key, i2)] = w_pair
         bias_bf = keep.tile([P, OUT], BF16, name="bias_bf")
-        nc.sync.dma_start(out=bias_bf[:], in_=b_ff.partition_broadcast(P))
 
         ident_bf = keep.tile([P, P], BF16, name="ident_bf")
         make_identity(nc, ident_bf[:])
@@ -56,6 +55,10 @@ def tile_differ_amplifier_pa_kernel(tc, h, w, w_ff, b_ff, out):
         make_identity(nc, ident_f32[:])
         ones = keep.tile([P, HID], BF16, name="ones")
         nc.vector.memset(ones[:], 1.0)
+        pows = keep.tile([P, 32], BF16, name="pows")
+        nc.vector.memset(pows[:], 0.0)
+        for z in range(4):
+            nc.vector.memset(pows[:, z : z + 1], -(2.0 ** (-10 * (z + 1))))
         warm_in = keep.tile([P, 1], F32, name="warm_in")
         nc.vector.memset(warm_in[:], 0.0)
         warm_out = keep.tile([P, 1], F32, name="warm_out")
@@ -66,8 +69,7 @@ def tile_differ_amplifier_pa_kernel(tc, h, w, w_ff, b_ff, out):
         warm_ps = psum.tile([P, HID], F32, tag="bank", name="warm_ps")
         for rep in range(4):
             nc.tensor.matmul(warm_ps[:], lhsT=ones[:, 0:P], rhs=ones[:], start=True, stop=True)
-        tot_ps = psum.tile([P, 96], F32, tag="bank", name="tot_ps")
-        tot_sb = keep.tile([P, 4], F32, name="tot_sb")
+        tot_ps = psum.tile([P, 160], F32, tag="bank", name="tot_ps")
         c_sb = keep.tile([P, 4], F32, name="c_sb")
         hT_ps = {}
         wT_ps = {}
@@ -100,9 +102,9 @@ def tile_differ_amplifier_pa_kernel(tc, h, w, w_ff, b_ff, out):
         def sums(q):
             for jj in range(2):
                 for t in range(4):
-                    col = 2 * (4 * (2 * q + jj) + t)
+                    col = 4 * (4 * (2 * q + jj) + t)
                     nc.tensor.matmul(
-                        tot_ps[:, col : col + 32], lhsT=h_sb[q][:, jj, t:HID:4], rhs=ones[:, 0:32], start=True, stop=True
+                        tot_ps[:, col : col + 32], lhsT=h_sb[q][:, jj, t:HID:4], rhs=pows[:], start=True, stop=True
                     )
 
         def turn_h(q):
@@ -113,9 +115,8 @@ def tile_differ_amplifier_pa_kernel(tc, h, w, w_ff, b_ff, out):
 
         def total():
             nc.vector.tensor_reduce(
-                out=tot_sb[:], in_=tot_ps[:, 0:64].rearrange("p (j t z) -> p t j z", t=4, z=2)[:, :, :, 0], axis=AX.X, op=ALU.add
+                out=c_sb[:], in_=tot_ps[:, 0:128].rearrange("p (j t z) -> p t j z", t=4, z=4), axis=AX.XY, op=ALU.add
             )
-            nc.vector.tensor_scalar_mul(out=c_sb[:], in0=tot_sb[:], scalar1=-1.0 / (N_ROWS - 1))
 
         def turn_w(key, i2):
             wT_ps[(key, i2)] = psum.tile([P, 2, W2], F32, tag="bank", name="wT_ps")
@@ -129,6 +130,9 @@ def tile_differ_amplifier_pa_kernel(tc, h, w, w_ff, b_ff, out):
         def copy_w(key, i2):
             wg[(key, i2)] = keep.tile([P, W2, 4], BF16, name="wg_%s%d" % (key, i2), align_bytes=64)
             nc.scalar.copy(out=wg[(key, i2)][:].bitcast(F32), in_=wT_ps[(key, i2)][:].rearrange("p u o -> p o u"))
+
+        def load_bias():
+            nc.scalar.dma_start(out=bias_bf[:], in_=b_ff.partition_broadcast(P))
 
         def quant_w(key, i2):
             cols = slice(i2 * W2, (i2 + 1) * W2)
@@ -251,23 +255,24 @@ def tile_differ_amplifier_pa_kernel(tc, h, w, w_ff, b_ff, out):
         copy_w("w", 0)
         turn_w("w", 1)
         copy_w("w", 1)
+        load_bias()
         centre(1)
+        turn_h(2)
         turn_h(3)
         centre_s(3)
-        turn_h(2)
         quant_w("w", 0)
-        quant_w("w", 1)
         quant_r(0)
+        quant_w("w", 1)
         centre(2)
         quant_r(1)
-        turn_w("f", 0)
-        copy_w("f", 0)
-        turn_w("f", 1)
-        copy_w("f", 1)
         mm1(0)
         mm1(1)
         mm1(2)
         mm1(3)
+        turn_w("f", 0)
+        copy_w("f", 0)
+        turn_w("f", 1)
+        copy_w("f", 1)
         add_h(0)
         add_h(1)
         quant_r(2)
@@ -277,13 +282,13 @@ def tile_differ_amplifier_pa_kernel(tc, h, w, w_ff, b_ff, out):
         copy_n(0)
         add_h(2)
         add_h(3)
-        quant_r(3)
-        mm1(6)
-        mm1(7)
         turn_n(1)
         copy_n(1)
         add_h(4)
         add_h(5)
+        quant_r(3)
+        mm1(6)
+        mm1(7)
         turn_n(2)
         copy_n(2)
         quant_w("f", 0)

from contextlib import ExitStack

import concourse.mybir as mybir
from concourse.masks import make_identity

N_ROWS, HID, OUT = 1024, 512, 512
FLOPS = 2 * N_ROWS * HID * HID + 2 * N_ROWS * HID * OUT

F32 = mybir.dt.float32
BF16 = mybir.dt.bfloat16
U32 = mybir.dt.uint32
U8 = mybir.dt.uint8
FP8X4 = mybir.dt.float8_e4m3fn_x4
ALU = mybir.AluOpType
ACT = mybir.ActivationFunctionType
AX = mybir.AxisListType

P = 128
NT = N_ROWS // P
NQ = NT // 2
W2 = 2 * P


def tile_differ_amplifier_pa_kernel(tc, h, w, w_ff, b_ff, out):
    nc = tc.nc
    with ExitStack() as ctx:
        keep = ctx.enter_context(tc.tile_pool(name="keep", bufs=1))
        work = ctx.enter_context(tc.tile_pool(name="work", bufs=4))
        psum = ctx.enter_context(tc.psum_pool(name="psum", bufs=8))

        h_view = h.rearrange("(p j) k -> p j k", j=NT)
        out_view = out.rearrange("(p j) o -> p j o", j=NT)

        h_sb = []
        for q in range(NQ):
            h_pair = keep.tile([P, 2, HID], BF16, name="h_sb%d" % q)
            if q < NQ - 1:
                nc.sync.dma_start(out=h_pair[:], in_=h_view[:, 2 * q : 2 * q + 2, :])
            else:
                for jj in range(2):
                    nc.sync.dma_start(out=h_pair[:, jj, :], in_=h_view[:, 2 * q + jj, :])
            h_sb.append(h_pair)
        wt_sb = {}
        for key, src in (("w", w), ("f", w_ff)):
            src_view = src.rearrange("(i p) k -> p i k", p=P)
            for i2 in range(2):
                w_pair = keep.tile([P, 2, HID], BF16, name="w_sb_%s%d" % (key, i2))
                nc.sync.dma_start(out=w_pair[:], in_=src_view[:, 2 * i2 : 2 * i2 + 2, :])
                wt_sb[(key, i2)] = w_pair
        bias_bf = keep.tile([P, OUT], BF16, name="bias_bf")

        ident_bf = keep.tile([P, P], BF16, name="ident_bf")
        make_identity(nc, ident_bf[:])
        ident_f32 = keep.tile([P, P], F32, name="ident_f32")
        make_identity(nc, ident_f32[:])
        ones = keep.tile([P, HID], BF16, name="ones")
        nc.vector.memset(ones[:], 1.0)
        pows = keep.tile([P, 32], BF16, name="pows")
        nc.vector.memset(pows[:], 0.0)
        for z in range(4):
            nc.vector.memset(pows[:, z : z + 1], -(2.0 ** (-10 * (z + 1))))
        warm_in = keep.tile([P, 1], F32, name="warm_in")
        nc.vector.memset(warm_in[:], 0.0)
        warm_out = keep.tile([P, 1], F32, name="warm_out")
        nc.scalar.activation(out=warm_out[:], in_=warm_in[:], func=ACT.Sigmoid)

        ctx.enter_context(tc.manual_schedule())

        warm_ps = psum.tile([P, HID], F32, tag="bank", name="warm_ps")
        for rep in range(4):
            nc.tensor.matmul(warm_ps[:], lhsT=ones[:, 0:P], rhs=ones[:], start=True, stop=True)
        tot_ps = psum.tile([P, 160], F32, tag="bank", name="tot_ps")
        c_sb = keep.tile([P, 4], F32, name="c_sb")
        hT_ps = {}
        wT_ps = {}
        wg = {}
        codes = {}
        scales = {}
        for key in ("w", "f"):
            codes[key] = keep.tile([P, HID], U32, name="codes_%s" % key, align_bytes=64)
            scales[key] = keep.tile([P, HID], U8, name="scales_%s" % key, align_bytes=64)
        rg = []
        r_codes = []
        r_scales = []
        hn = []
        hng = []
        n_codes = []
        n_scales = []
        for q in range(NQ):
            rg.append(keep.tile([P, W2, 4], BF16, name="rg%d" % q, align_bytes=64))
            r_codes.append(keep.tile([P, W2], U32, name="r_codes%d" % q, align_bytes=64))
            r_scales.append(keep.tile([P, W2], U8, name="r_scales%d" % q, align_bytes=64))
            hn.append(keep.tile([P, 2, HID], BF16, name="hn%d" % q))
            hng.append(keep.tile([P, W2, 4], BF16, name="hng%d" % q, align_bytes=64))
            n_codes.append(keep.tile([P, W2], U32, name="n_codes%d" % q, align_bytes=64))
            n_scales.append(keep.tile([P, W2], U8, name="n_scales%d" % q, align_bytes=64))
        f_ps = {}
        hnT_ps = {}
        o_ps = {}
        z_sb = {}

        def sums(q):
            for jj in range(2):
                for t in range(4):
                    col = 4 * (4 * (2 * q + jj) + t)
                    nc.tensor.matmul(
                        tot_ps[:, col : col + 32], lhsT=h_sb[q][:, jj, t:HID:4], rhs=pows[:], start=True, stop=True
                    )

        def turn_h(q):
            hT_ps[q] = psum.tile([P, 4, W2], BF16, tag="bank", name="hT_ps")
            for jj in range(2):
                for t in range(4):
                    nc.tensor.transpose(hT_ps[q][:, t, jj * P : (jj + 1) * P], h_sb[q][:, jj, t:HID:4], ident_bf[:])

        def total():
            nc.vector.tensor_reduce(
                out=c_sb[:], in_=tot_ps[:, 0:128].rearrange("p (j t z) -> p t j z", t=4, z=4), axis=AX.XY, op=ALU.add
            )

        def turn_w(key, i2):
            wT_ps[(key, i2)] = psum.tile([P, 2, W2], F32, tag="bank", name="wT_ps")
            for i in range(2):
                words = wt_sb[(key, i2)][:, i, :].bitcast(F32)
                for u in range(2):
                    nc.tensor.transpose(
                        wT_ps[(key, i2)][:, u, i * P : (i + 1) * P], words[:, u : HID // 2 : 2], ident_f32[:]
                    )

        def copy_w(key, i2):
            wg[(key, i2)] = keep.tile([P, W2, 4], BF16, name="wg_%s%d" % (key, i2), align_bytes=64)
            nc.scalar.copy(out=wg[(key, i2)][:].bitcast(F32), in_=wT_ps[(key, i2)][:].rearrange("p u o -> p o u"))

        def load_bias():
            nc.scalar.dma_start(out=bias_bf[:], in_=b_ff.partition_broadcast(P))

        def quant_w(key, i2):
            cols = slice(i2 * W2, (i2 + 1) * W2)
            nc.vector.quantize_mx(
                out=codes[key][:, cols].bitcast(FP8X4),
                scales=scales[key][:, cols],
                in_=wg[(key, i2)][:].rearrange("p o t -> p (o t)"),
            )

        def centre(q):
            nc.vector.scalar_tensor_tensor(
                out=rg[q][:],
                in0=hT_ps[q][:].rearrange("p t n -> p n t"),
                scalar=float(N_ROWS) / (N_ROWS - 1),
                in1=c_sb[:].unsqueeze(1).to_broadcast([P, W2, 4]),
                op0=ALU.mult,
                op1=ALU.add,
            )

        def centre_s(q):
            for t in range(4):
                nc.scalar.activation(
                    out=rg[q][:, :, t],
                    in_=hT_ps[q][:, t, :],
                    func=ACT.Identity,
                    scale=float(N_ROWS) / (N_ROWS - 1),
                    bias=c_sb[:, t : t + 1],
                )

        def quant_r(q):
            nc.vector.quantize_mx(
                out=r_codes[q][:].bitcast(FP8X4), scales=r_scales[q][:], in_=rg[q][:].rearrange("p n t -> p (n t)")
            )

        def mm1(j):
            q, jj = divmod(j, 2)
            rows = slice(jj * P, (jj + 1) * P)
            f_ps[j] = psum.tile([P, HID], F32, tag="bank", name="f_ps")
            nc.tensor.matmul_mx(
                out=f_ps[j][:],
                lhsT=r_codes[q][:, rows].bitcast(FP8X4),
                lhsT_scale=r_scales[q][:, rows],
                rhs=codes["w"][:].bitcast(FP8X4),
                rhs_scale=scales["w"][:],
                start=True,
                stop=True,
            )

        def add_h(j):
            q, jj = divmod(j, 2)
            nc.vector.tensor_tensor(out=hn[q][:, jj, :], in0=f_ps[j][:], in1=h_sb[q][:, jj, :], op=ALU.add)

        def turn_n(q):
            hnT_ps[q] = psum.tile([P, 2, W2], F32, tag="bank", name="hnT_ps")
            for jj in range(2):
                words = hn[q][:, jj, :].bitcast(F32)
                for u in range(2):
                    nc.tensor.transpose(hnT_ps[q][:, u, jj * P : (jj + 1) * P], words[:, u : HID // 2 : 2], ident_f32[:])

        def copy_n(q):
            nc.scalar.copy(out=hng[q][:].bitcast(F32), in_=hnT_ps[q][:].rearrange("p u n -> p n u"))

        def quant_n(q):
            nc.vector.quantize_mx(
                out=n_codes[q][:].bitcast(FP8X4), scales=n_scales[q][:], in_=hng[q][:].rearrange("p n t -> p (n t)")
            )

        def turn_n1(j):
            q, jj = divmod(j, 2)
            hnT_ps[(q, jj)] = psum.tile([P, 2, P], F32, tag="bank", name="hnT1_ps")
            words = hn[q][:, jj, :].bitcast(F32)
            for u in range(2):
                nc.tensor.transpose(hnT_ps[(q, jj)][:, u, :], words[:, u : HID // 2 : 2], ident_f32[:])

        def copy_n1(j):
            q, jj = divmod(j, 2)
            nc.scalar.copy(
                out=hng[q][:, jj * P : (jj + 1) * P, :].bitcast(F32), in_=hnT_ps[(q, jj)][:].rearrange("p u n -> p n u")
            )

        def quant_n1(j):
            q, jj = divmod(j, 2)
            rows = slice(jj * P, (jj + 1) * P)
            nc.vector.quantize_mx(
                out=n_codes[q][:, rows].bitcast(FP8X4),
                scales=n_scales[q][:, rows],
                in_=hng[q][:, rows, :].rearrange("p n t -> p (n t)"),
            )

        def mm2(j):
            q, jj = divmod(j, 2)
            rows = slice(jj * P, (jj + 1) * P)
            o_ps[j] = psum.tile([P, OUT], F32, tag="bank", name="o_ps")
            nc.tensor.matmul_mx(
                out=o_ps[j][:],
                lhsT=n_codes[q][:, rows].bitcast(FP8X4),
                lhsT_scale=n_scales[q][:, rows],
                rhs=codes["f"][:].bitcast(FP8X4),
                rhs_scale=scales["f"][:],
                start=True,
                stop=True,
            )

        def finish(j, c0=0, c1=OUT):
            z = keep.tile([P, c1 - c0], F32, name="z%d_%d" % (j, c0))
            nc.vector.tensor_tensor(out=z[:], in0=o_ps[j][:, c0:c1], in1=bias_bf[:, c0:c1], op=ALU.add)
            y = keep.tile([P, c1 - c0], F32, name="y%d_%d" % (j, c0))
            nc.scalar.activation(out=y[:], in_=z[:], func=ACT.Sigmoid)
            nc.sync.dma_start(out=out_view[:, j, c0:c1], in_=y[:])

        sums(0)
        sums(1)
        turn_h(0)
        sums(2)
        sums(3)
        total()
        turn_h(1)
        centre(0)
        turn_w("w", 0)
        copy_w("w", 0)
        turn_w("w", 1)
        copy_w("w", 1)
        load_bias()
        centre(1)
        turn_h(2)
        turn_h(3)
        centre_s(3)
        quant_w("w", 0)
        quant_r(0)
        quant_w("w", 1)
        centre(2)
        quant_r(1)
        mm1(0)
        mm1(1)
        mm1(2)
        mm1(3)
        turn_w("f", 0)
        copy_w("f", 0)
        turn_w("f", 1)
        copy_w("f", 1)
        add_h(0)
        add_h(1)
        quant_r(2)
        mm1(4)
        mm1(5)
        turn_n(0)
        copy_n(0)
        add_h(2)
        add_h(3)
        turn_n(1)
        copy_n(1)
        add_h(4)
        add_h(5)
        quant_r(3)
        mm1(6)
        mm1(7)
        turn_n(2)
        copy_n(2)
        quant_w("f", 0)
        quant_w("f", 1)
        quant_n(0)
        mm2(0)
        mm2(1)
        add_h(6)
        turn_n1(6)
        copy_n1(6)
        add_h(7)
        turn_n1(7)
        copy_n1(7)
        quant_n(1)
        mm2(2)
        mm2(3)
        finish(0)
        finish(1)
        quant_n(2)
        quant_n1(6)
        mm2(4)
        mm2(5)
        finish(2)
        quant_n1(7)
        mm2(6)
        mm2(7)
        finish(3)
        finish(4)
        finish(5)
        finish(6)
        finish(7, 0, OUT // 2)
        finish(7, OUT // 2, OUT)
